import numpy as np
import ml_dtypes


def mxq(x, axis, fmt="e4m3"):
    dtype, down = {"e4m3": (ml_dtypes.float8_e4m3fn, 7), "e5m2": (ml_dtypes.float8_e5m2, 14)}[fmt]
    v = np.moveaxis(np.asarray(x, np.float32).astype(ml_dtypes.bfloat16).astype(np.float64), axis, -1)
    blocks = v.reshape(v.shape[:-1] + (-1, 32))
    amax = np.abs(blocks).max(-1, keepdims=True)
    byte = np.maximum(np.where(amax > 0, np.frexp(amax)[1] - 1 + 127, 0) - down, 1)
    scale = np.exp2(byte - 127.0)
    codes = (blocks / scale).astype(np.float32).astype(dtype).astype(np.float64)
    return np.moveaxis((codes * scale).reshape(v.shape), -1, axis)


WIDE = False


def mx_kscale(k):
    if not WIDE:
        return np.ones(k)
    levels = np.array([10, -10, 5, -5, 0])
    a = np.random.permutation(np.resize(levels, k // 512 * 4)).reshape(k // 512, 4)
    idx = np.arange(k)
    return np.exp2(a[idx // 512, idx % 128 // 32])


BF16 = ml_dtypes.bfloat16


def bf(x):
    return np.asarray(x, np.float32).astype(BF16)


def f64(x):
    return np.asarray(x).astype(np.float64)


B, S, HIDDEN, NUM_HEADS, HEAD_DIM = 2, 64, 512, 16, 64
F = NUM_HEADS * HEAD_DIM


def _split_heads(x):
    b, s, _ = x.shape
    return x.reshape(b, s, NUM_HEADS, HEAD_DIM).transpose(0, 2, 1, 3)


def setup_inputs():
    s = mx_kscale(HIDDEN)
    scale = 1.0 / np.sqrt(HIDDEN)
    return {
        "hidden_states": bf(np.random.standard_normal((B, S, HIDDEN)) * s),
        "Wq": bf(np.random.standard_normal((HIDDEN, F)) * scale / s[:, None]),
        "bq": bf(np.random.standard_normal(F) * 0.5),
        "Wk": bf(np.random.standard_normal((HIDDEN, F)) * scale / s[:, None]),
        "bk": bf(np.random.standard_normal(F) * 0.5),
        "Wv": bf(np.random.standard_normal((HIDDEN, F)) * scale / s[:, None]),
        "bv": bf(np.random.standard_normal(F) * 0.5),
    }


def reference(hidden_states, Wq, bq, Wk, bk, Wv, bv):
    Wqkv = np.concatenate([f64(Wq), f64(Wk), f64(Wv)], axis=1)
    bqkv = np.concatenate([f64(bq), f64(bk), f64(bv)], axis=0)
    qkv = (mxq(f64(hidden_states), 2, "e4m3") @ mxq(Wqkv, 0, "e4m3")) + bqkv
    q, k, v = np.split(qkv, 3, axis=-1)
    return (_split_heads(q), _split_heads(k), _split_heads(v))

@@ -1,0 +1,156 @@
+from contextlib import ExitStack
+
+import concourse.masks as masks
+import concourse.mybir as mybir
+
+BF16 = mybir.dt.bfloat16
+F32 = mybir.dt.float32
+U32 = mybir.dt.uint32
+U8 = mybir.dt.uint8
+FP8X4 = mybir.dt.float8_e4m3fn_x4
+
+P = 128
+PACK = 4
+BATCH, SEQ, HIDDEN = 2, 64, 512
+HEADS, HEAD_DIM = 16, 64
+WIDTH = HEADS * HEAD_DIM
+TOKENS = BATCH * SEQ
+N_TILE = 512
+TILES_PER_MATRIX = WIDTH // N_TILE
+HEADS_PER_TILE = N_TILE // HEAD_DIM
+BIAS_ROWS = WIDTH // P
+RUN = 4
+
+VECTOR_COLS = 192
+
+assert HIDDEN == P * PACK and TOKENS == P
+
+FLOPS = 2 * TOKENS * HIDDEN * 3 * WIDTH
+
+
+def tile_attention_before_s_kernel(
+    tc, hidden_states, Wq, bq, Wk, bk, Wv, bv, out_0, out_1, out_2
+):
+    nc = tc.nc
+    weights = (Wq, Wk, Wv)
+    biases = (bq, bk, bv)
+    outs = (out_0, out_1, out_2)
+    n_tiles = len(weights) * TILES_PER_MATRIX
+
+    with ExitStack() as ctx:
+        keep = ctx.enter_context(tc.tile_pool(name="keep", bufs=1))
+        stream = ctx.enter_context(tc.tile_pool(name="stream", bufs=n_tiles))
+        psum_prep = ctx.enter_context(tc.psum_pool(name="psum_prep", bufs=1))
+        psum_bias = ctx.enter_context(tc.psum_pool(name="psum_bias", bufs=2))
+        psum_acc = ctx.enter_context(tc.psum_pool(name="psum_acc", bufs=4))
+
+        x_sb = keep.tile([P, HIDDEN], BF16)
+        nc.sync.dma_start(out=x_sb[:], in_=hidden_states.rearrange("b s k -> (b s) k"))
+
+        raw_tiles = []
+        for i in range(n_tiles):
+            w_rows = weights[i // TILES_PER_MATRIX].rearrange("(p j) n -> p j n", j=PACK)
+            first = (i % TILES_PER_MATRIX) * N_TILE
+            raw = stream.tile([P, PACK, N_TILE], BF16)
+            nc.sync.dma_start(out=raw[:], in_=w_rows[:, :, first : first + N_TILE])
+            raw_tiles.append(raw)
+
+        bias_rows = keep.tile([P, P], BF16)
+        nc.vector.memset(bias_rows[:], 0.0)
+        for t, bias in enumerate(biases):
+            nc.scalar.dma_start(
+                out=bias_rows[t * BIAS_ROWS : (t + 1) * BIAS_ROWS, :],
+                in_=bias.rearrange("(r c) -> r c", c=P),
+            )
+
+        ident_f32 = keep.tile([P, P], F32)
+        masks.make_identity(nc, ident_f32[:])
+        ident_bf16 = keep.tile([P, P], BF16)
+        masks.make_identity(nc, ident_bf16[:])
+
+        x_words = x_sb[:].bitcast(F32).rearrange("t (p u) -> t u p", u=2)
+        x_t = psum_prep.tile([P, 2, TOKENS], F32)
+        for u in range(2):
+            nc.tensor.transpose(x_t[:, u, :], x_words[:, u, :], ident_f32[:])
+        x_grouped = keep.tile([P, TOKENS * PACK], BF16, align_bytes=64)
+        nc.vector.tensor_copy(
+            out=x_grouped[:].bitcast(F32).rearrange("p (t u) -> p t u", u=2),
+            in_=x_t[:].rearrange("p u t -> p t u"),
+        )
+        x_codes = keep.tile([P, TOKENS], U32, align_bytes=64)
+        x_scales = keep.tile([P, TOKENS], U8, align_bytes=64)
+        nc.vector.quantize_mx(out=x_codes[:].bitcast(FP8X4), scales=x_scales[:], in_=x_grouped[:])
+
+        bias_t = psum_prep.tile([P, P], BF16)
+        nc.tensor.transpose(bias_t[:], bias_rows[:], ident_bf16[:])
+        bias_cols = keep.tile([P, len(biases) * BIAS_ROWS], BF16)
+        nc.scalar.copy(out=bias_cols[:], in_=bias_t[:, 0 : len(biases) * BIAS_ROWS])
+        bias_all = keep.tile([P, len(biases), WIDTH], BF16)
+        for t in range(len(biases)):
+            spread = psum_bias.tile([P, WIDTH], BF16)
+            for r in range(BIAS_ROWS):
+                column = bias_cols[:, t * BIAS_ROWS + r : t * BIAS_ROWS + r + 1]
+                nc.tensor.transpose(
+                    spread[:, r * P : (r + 1) * P], column.to_broadcast([P, P]), ident_bf16[:]
+                )
+            nc.scalar.copy(out=bias_all[:, t, :], in_=spread[:])
+
+        grouped_tiles = []
+        acc_tiles = []
+
+        def regroup(i):
+            grouped = stream.tile([P, N_TILE, PACK], BF16, align_bytes=64)
+            for copy, cols in (
+                (nc.vector.tensor_copy, slice(0, VECTOR_COLS)),
+                (nc.scalar.copy, slice(VECTOR_COLS, N_TILE)),
+            ):
+                copy(
+                    out=grouped[:, cols, :].rearrange("p (c i) j -> p c j i", i=RUN),
+                    in_=raw_tiles[i][:, :, cols].rearrange("p j (c i) -> p c j i", i=RUN),
+                )
+            grouped_tiles.append(grouped)
+
+        def quantise_and_multiply(i):
+            codes = stream.tile([P, N_TILE], U32, align_bytes=64)
+            scales = stream.tile([P, N_TILE], U8, align_bytes=64)
+            nc.vector.quantize_mx(
+                out=codes[:].bitcast(FP8X4),
+                scales=scales[:],
+                in_=grouped_tiles[i][:].rearrange("p n j -> p (n j)"),
+            )
+            acc = psum_acc.tile([P, N_TILE], F32)
+            nc.tensor.matmul_mx(
+                out=acc[:],
+                lhsT=x_codes[:].bitcast(FP8X4),
+                lhsT_scale=x_scales[:],
+                rhs=codes[:].bitcast(FP8X4),
+                rhs_scale=scales[:],
+                start=True,
+                stop=True,
+            )
+            acc_tiles.append(acc)
+
+        def add_bias_and_store(i):
+            t = i // TILES_PER_MATRIX
+            half = i % TILES_PER_MATRIX
+            result = stream.tile([P, N_TILE], F32)
+            nc.vector.tensor_tensor(
+                out=result[:],
+                in0=acc_tiles[i][:],
+                in1=bias_all[:, t, half * N_TILE : (half + 1) * N_TILE],
+                op=mybir.AluOpType.add,
+            )
+            heads = slice(half * HEADS_PER_TILE, (half + 1) * HEADS_PER_TILE)
+            for b in range(BATCH):
+                nc.sync.dma_start(
+                    out=outs[t][b, heads, :, :].rearrange("h s d -> s h d"),
+                    in_=result[b * SEQ : (b + 1) * SEQ, :].rearrange("s (h d) -> s h d", d=HEAD_DIM),
+                )
+
+        for step in range(n_tiles + 2):
+            if step < n_tiles:
+                regroup(step)
+            if 1 <= step <= n_tiles:
+                quantise_and_multiply(step - 1)
+            if step >= 2:
+                add_bias_and_store(step - 2)

@@ -45,7 +45,7 @@ def tile_attention_before_s_kernel(
         psum_acc = ctx.enter_context(tc.psum_pool(name="psum_acc", bufs=4))
 
         x_sb = keep.tile([P, HIDDEN], BF16)
-        nc.sync.dma_start(out=x_sb[:], in_=hidden_states.rearrange("b s k -> (b s) k"))
+        nc.sync.dma_start(out=x_sb[:], in_=hidden_states.rearrange("b s k -> s b k"))
 
         raw_tiles = []
         for i in range(n_tiles):
@@ -144,7 +144,7 @@ def tile_attention_before_s_kernel(
             for b in range(BATCH):
                 nc.sync.dma_start(
                     out=outs[t][b, heads, :, :].rearrange("h s d -> s h d"),
-                    in_=result[b * SEQ : (b + 1) * SEQ, :].rearrange("s (h d) -> s h d", d=HEAD_DIM),
+                    in_=result[b:P:BATCH, :].rearrange("s (h d) -> s h d", d=HEAD_DIM),
                 )
 
         for step in range(n_tiles + 2):

@@ -17,13 +17,14 @@ WIDTH = HEADS * HEAD_DIM
 TOKENS = BATCH * SEQ
 N_TILE = 512
 TILES_PER_MATRIX = WIDTH // N_TILE
-HEADS_PER_TILE = N_TILE // HEAD_DIM
 BIAS_ROWS = WIDTH // P
 RUN = 4
 
-VECTOR_COLS = 192
+LAST_TILE_PIECES = (256, 128, 128)
 
-assert HIDDEN == P * PACK and TOKENS == P
+VECTOR_EIGHTHS = 3
+
+assert HIDDEN == P * PACK and TOKENS == P and sum(LAST_TILE_PIECES) == N_TILE
 
 FLOPS = 2 * TOKENS * HIDDEN * 3 * WIDTH
 
@@ -37,23 +38,33 @@ def tile_attention_before_s_kernel(
     outs = (out_0, out_1, out_2)
     n_tiles = len(weights) * TILES_PER_MATRIX
 
+    pieces = [(i, 0, N_TILE) for i in range(n_tiles - 1)]
+    for j, width in enumerate(LAST_TILE_PIECES):
+        pieces.append((n_tiles - 1, sum(LAST_TILE_PIECES[:j]), width))
+    n_pieces = len(pieces)
+
     with ExitStack() as ctx:
         keep = ctx.enter_context(tc.tile_pool(name="keep", bufs=1))
-        stream = ctx.enter_context(tc.tile_pool(name="stream", bufs=n_tiles))
+        stream = ctx.enter_context(tc.tile_pool(name="stream", bufs=n_pieces))
         psum_prep = ctx.enter_context(tc.psum_pool(name="psum_prep", bufs=1))
         psum_bias = ctx.enter_context(tc.psum_pool(name="psum_bias", bufs=2))
         psum_acc = ctx.enter_context(tc.psum_pool(name="psum_acc", bufs=4))
-
-        x_sb = keep.tile([P, HIDDEN], BF16)
-        nc.sync.dma_start(out=x_sb[:], in_=hidden_states.rearrange("b s k -> s b k"))
+        ctx.enter_context(tc.manual_schedule())
 
         raw_tiles = []
-        for i in range(n_tiles):
+
+        def load_weight_tile(i):
             w_rows = weights[i // TILES_PER_MATRIX].rearrange("(p j) n -> p j n", j=PACK)
             first = (i % TILES_PER_MATRIX) * N_TILE
             raw = stream.tile([P, PACK, N_TILE], BF16)
             nc.sync.dma_start(out=raw[:], in_=w_rows[:, :, first : first + N_TILE])
             raw_tiles.append(raw)
+
+        load_weight_tile(0)
+        x_sb = keep.tile([P, HIDDEN], BF16)
+        nc.sync.dma_start(out=x_sb[:], in_=hidden_states.rearrange("b s k -> s b k"))
+        for i in range(1, n_tiles):
+            load_weight_tile(i)
 
         bias_rows = keep.tile([P, P], BF16)
         nc.vector.memset(bias_rows[:], 0.0)
@@ -63,30 +74,18 @@ def tile_attention_before_s_kernel(
                 in_=bias.rearrange("(r c) -> r c", c=P),
             )
 
-        ident_f32 = keep.tile([P, P], F32)
-        masks.make_identity(nc, ident_f32[:])
         ident_bf16 = keep.tile([P, P], BF16)
         masks.make_identity(nc, ident_bf16[:])
-
-        x_words = x_sb[:].bitcast(F32).rearrange("t (p u) -> t u p", u=2)
-        x_t = psum_prep.tile([P, 2, TOKENS], F32)
-        for u in range(2):
-            nc.tensor.transpose(x_t[:, u, :], x_words[:, u, :], ident_f32[:])
-        x_grouped = keep.tile([P, TOKENS * PACK], BF16, align_bytes=64)
-        nc.vector.tensor_copy(
-            out=x_grouped[:].bitcast(F32).rearrange("p (t u) -> p t u", u=2),
-            in_=x_t[:].rearrange("p u t -> p t u"),
-        )
-        x_codes = keep.tile([P, TOKENS], U32, align_bytes=64)
-        x_scales = keep.tile([P, TOKENS], U8, align_bytes=64)
-        nc.vector.quantize_mx(out=x_codes[:].bitcast(FP8X4), scales=x_scales[:], in_=x_grouped[:])
+        ident_f32 = keep.tile([P, P], F32)
+        masks.make_identity(nc, ident_f32[:])
 
         bias_t = psum_prep.tile([P, P], BF16)
         nc.tensor.transpose(bias_t[:], bias_rows[:], ident_bf16[:])
         bias_cols = keep.tile([P, len(biases) * BIAS_ROWS], BF16)
-        nc.scalar.copy(out=bias_cols[:], in_=bias_t[:, 0 : len(biases) * BIAS_ROWS])
+        nc.vector.tensor_copy(out=bias_cols[:], in_=bias_t[:, 0 : len(biases) * BIAS_ROWS])
         bias_all = keep.tile([P, len(biases), WIDTH], BF16)
-        for t in range(len(biases)):
+
+        def spread_bias(t):
             spread = psum_bias.tile([P, WIDTH], BF16)
             for r in range(BIAS_ROWS):
                 column = bias_cols[:, t * BIAS_ROWS + r : t * BIAS_ROWS + r + 1]
@@ -95,30 +94,52 @@ def tile_attention_before_s_kernel(
                 )
             nc.scalar.copy(out=bias_all[:, t, :], in_=spread[:])
 
+        x_codes = keep.tile([P, TOKENS], U32, align_bytes=64)
+        x_scales = keep.tile([P, TOKENS], U8, align_bytes=64)
+
+        def quantise_tokens():
+            x_words = x_sb[:].bitcast(F32).rearrange("t (p u) -> t u p", u=2)
+            x_t = psum_prep.tile([P, 2, TOKENS], F32)
+            for u in range(2):
+                nc.tensor.transpose(x_t[:, u, :], x_words[:, u, :], ident_f32[:])
+            x_grouped = keep.tile([P, TOKENS * PACK], BF16, align_bytes=64)
+            nc.vector.tensor_copy(
+                out=x_grouped[:].bitcast(F32).rearrange("p (t u) -> p t u", u=2),
+                in_=x_t[:].rearrange("p u t -> p t u"),
+            )
+            nc.vector.quantize_mx(
+                out=x_codes[:].bitcast(FP8X4), scales=x_scales[:], in_=x_grouped[:]
+            )
+
         grouped_tiles = []
         acc_tiles = []
 
-        def regroup(i):
-            grouped = stream.tile([P, N_TILE, PACK], BF16, align_bytes=64)
-            for copy, cols in (
-                (nc.vector.tensor_copy, slice(0, VECTOR_COLS)),
-                (nc.scalar.copy, slice(VECTOR_COLS, N_TILE)),
+        def regroup(n):
+            i, first, width = pieces[n]
+            vector_cols = width * VECTOR_EIGHTHS // 8
+            grouped = stream.tile([P, width, PACK], BF16, align_bytes=64)
+            for copy, lo, hi in (
+                (nc.vector.tensor_copy, 0, vector_cols),
+                (nc.scalar.copy, vector_cols, width),
             ):
                 copy(
-                    out=grouped[:, cols, :].rearrange("p (c i) j -> p c j i", i=RUN),
-                    in_=raw_tiles[i][:, :, cols].rearrange("p j (c i) -> p c j i", i=RUN),
+                    out=grouped[:, lo:hi, :].rearrange("p (c i) j -> p c j i", i=RUN),
+                    in_=raw_tiles[i][:, :, first + lo : first + hi].rearrange(
+                        "p j (c i) -> p c j i", i=RUN
+                    ),
                 )
             grouped_tiles.append(grouped)
 
-        def quantise_and_multiply(i):
-            codes = stream.tile([P, N_TILE], U32, align_bytes=64)
-            scales = stream.tile([P, N_TILE], U8, align_bytes=64)
+        def quantise_and_multiply(n):
+            width = pieces[n][2]
+            codes = stream.tile([P, width], U32, align_bytes=64)
+            scales = stream.tile([P, width], U8, align_bytes=64)
             nc.vector.quantize_mx(
                 out=codes[:].bitcast(FP8X4),
                 scales=scales[:],
-                in_=grouped_tiles[i][:].rearrange("p n j -> p (n j)"),
+                in_=grouped_tiles[n][:].rearrange("p n j -> p (n j)"),
             )
-            acc = psum_acc.tile([P, N_TILE], F32)
+            acc = psum_acc.tile([P, width], F32)
             nc.tensor.matmul_mx(
                 out=acc[:],
                 lhsT=x_codes[:].bitcast(FP8X4),
@@ -130,27 +151,33 @@ def tile_attention_before_s_kernel(
             )
             acc_tiles.append(acc)
 
-        def add_bias_and_store(i):
+        def add_bias_and_store(n):
+            i, first, width = pieces[n]
             t = i // TILES_PER_MATRIX
-            half = i % TILES_PER_MATRIX
-            result = stream.tile([P, N_TILE], F32)
+            column = (i % TILES_PER_MATRIX) * N_TILE + first
+            result = stream.tile([P, width], F32)
             nc.vector.tensor_tensor(
                 out=result[:],
-                in0=acc_tiles[i][:],
-                in1=bias_all[:, t, half * N_TILE : (half + 1) * N_TILE],
+                in0=acc_tiles[n][:],
+                in1=bias_all[:, t, column : column + width],
                 op=mybir.AluOpType.add,
             )
-            heads = slice(half * HEADS_PER_TILE, (half + 1) * HEADS_PER_TILE)
+            heads = slice(column // HEAD_DIM, (column + width) // HEAD_DIM)
             for b in range(BATCH):
                 nc.sync.dma_start(
                     out=outs[t][b, heads, :, :].rearrange("h s d -> s h d"),
                     in_=result[b:P:BATCH, :].rearrange("s (h d) -> s h d", d=HEAD_DIM),
                 )
 
-        for step in range(n_tiles + 2):
-            if step < n_tiles:
+        regroup(0)
+        spread_bias(0)
+        quantise_tokens()
+        for step in range(1, n_pieces + 2):
+            if step < n_pieces:
                 regroup(step)
-            if 1 <= step <= n_tiles:
+            if step < len(biases):
+                spread_bias(step)
+            if step - 1 < n_pieces:
                 quantise_and_multiply(step - 1)
             if step >= 2:
                 add_bias_and_store(step - 2)

@@ -51,20 +51,18 @@ def tile_attention_before_s_kernel(
         psum_acc = ctx.enter_context(tc.psum_pool(name="psum_acc", bufs=4))
         ctx.enter_context(tc.manual_schedule())
 
-        raw_tiles = []
+        raw_matrices = []
 
-        def load_weight_tile(i):
-            w_rows = weights[i // TILES_PER_MATRIX].rearrange("(p j) n -> p j n", j=PACK)
-            first = (i % TILES_PER_MATRIX) * N_TILE
-            raw = stream.tile([P, PACK, N_TILE], BF16)
-            nc.sync.dma_start(out=raw[:], in_=w_rows[:, :, first : first + N_TILE])
-            raw_tiles.append(raw)
+        def load_matrix(t):
+            raw = keep.tile([P, PACK, WIDTH], BF16, name="raw%d" % t)
+            nc.sync.dma_start(out=raw[:], in_=weights[t].rearrange("(p j) n -> p j n", j=PACK))
+            raw_matrices.append(raw)
 
-        load_weight_tile(0)
+        load_matrix(0)
         x_sb = keep.tile([P, HIDDEN], BF16)
         nc.sync.dma_start(out=x_sb[:], in_=hidden_states.rearrange("b s k -> s b k"))
-        for i in range(1, n_tiles):
-            load_weight_tile(i)
+        for t in range(1, len(weights)):
+            load_matrix(t)
 
         bias_rows = keep.tile([P, P], BF16)
         nc.vector.memset(bias_rows[:], 0.0)
@@ -117,6 +115,8 @@ def tile_attention_before_s_kernel(
         def regroup(n):
             i, first, width = pieces[n]
             vector_cols = width * VECTOR_EIGHTHS // 8
+            raw = raw_matrices[i // TILES_PER_MATRIX]
+            first += (i % TILES_PER_MATRIX) * N_TILE
             grouped = stream.tile([P, width, PACK], BF16, align_bytes=64)
             for copy, lo, hi in (
                 (nc.vector.tensor_copy, 0, vector_cols),
@@ -124,7 +124,7 @@ def tile_attention_before_s_kernel(
             ):
                 copy(
                     out=grouped[:, lo:hi, :].rearrange("p (c i) j -> p c j i", i=RUN),
-                    in_=raw_tiles[i][:, :, first + lo : first + hi].rearrange(
+                    in_=raw[:, :, first + lo : first + hi].rearrange(
                         "p j (c i) -> p c j i", i=RUN
                     ),
                 )

@@ -16,15 +16,16 @@ HEADS, HEAD_DIM = 16, 64
 WIDTH = HEADS * HEAD_DIM
 TOKENS = BATCH * SEQ
 N_TILE = 512
-TILES_PER_MATRIX = WIDTH // N_TILE
 BIAS_ROWS = WIDTH // P
 RUN = 4
 
-LAST_TILE_PIECES = (256, 128, 128)
+LOAD_WIDTHS = ((256, 256, 512), (512, 512), (512, 512))
+
+PIECE_WIDTHS = ((256, 256, 512), (512, 512), (512, 256, 128, 128))
 
 VECTOR_EIGHTHS = 3
 
-assert HIDDEN == P * PACK and TOKENS == P and sum(LAST_TILE_PIECES) == N_TILE
+assert HIDDEN == P * PACK and TOKENS == P
 
 FLOPS = 2 * TOKENS * HIDDEN * 3 * WIDTH
 
@@ -36,12 +37,13 @@ def tile_attention_before_s_kernel(
     weights = (Wq, Wk, Wv)
     biases = (bq, bk, bv)
     outs = (out_0, out_1, out_2)
-    n_tiles = len(weights) * TILES_PER_MATRIX
 
-    pieces = [(i, 0, N_TILE) for i in range(n_tiles - 1)]
-    for j, width in enumerate(LAST_TILE_PIECES):
-        pieces.append((n_tiles - 1, sum(LAST_TILE_PIECES[:j]), width))
+    pieces = []
+    for t, widths in enumerate(PIECE_WIDTHS):
+        for j, width in enumerate(widths):
+            pieces.append((t, sum(widths[:j]), width))
     n_pieces = len(pieces)
+    first_piece = [sum(len(w) for w in PIECE_WIDTHS[:t]) for t in range(len(weights))]
 
     with ExitStack() as ctx:
         keep = ctx.enter_context(tc.tile_pool(name="keep", bufs=1))
@@ -51,26 +53,26 @@ def tile_attention_before_s_kernel(
         psum_acc = ctx.enter_context(tc.psum_pool(name="psum_acc", bufs=4))
         ctx.enter_context(tc.manual_schedule())
 
-        raw_matrices = []
-
-        def load_matrix(t):
-            raw = keep.tile([P, PACK, WIDTH], BF16, name="raw%d" % t)
-            nc.sync.dma_start(out=raw[:], in_=weights[t].rearrange("(p j) n -> p j n", j=PACK))
-            raw_matrices.append(raw)
-
-        load_matrix(0)
-        x_sb = keep.tile([P, HIDDEN], BF16)
-        nc.sync.dma_start(out=x_sb[:], in_=hidden_states.rearrange("b s k -> s b k"))
-        for t in range(1, len(weights)):
-            load_matrix(t)
-
         bias_rows = keep.tile([P, P], BF16)
         nc.vector.memset(bias_rows[:], 0.0)
         for t, bias in enumerate(biases):
-            nc.scalar.dma_start(
+            nc.sync.dma_start(
                 out=bias_rows[t * BIAS_ROWS : (t + 1) * BIAS_ROWS, :],
                 in_=bias.rearrange("(r c) -> r c", c=P),
             )
+        x_sb = keep.tile([P, HIDDEN], BF16)
+        nc.sync.dma_start(out=x_sb[:], in_=hidden_states.rearrange("b s k -> s b k"))
+        loads = []
+        for t, widths in enumerate(LOAD_WIDTHS):
+            loads.append([])
+            for j, width in enumerate(widths):
+                first = sum(widths[:j])
+                raw = keep.tile([P, PACK, width], BF16, name="raw%d_%d" % (t, j))
+                nc.sync.dma_start(
+                    out=raw[:],
+                    in_=weights[t][:, first : first + width].rearrange("(p j) n -> p j n", j=PACK),
+                )
+                loads[t].append((first, width, raw))
 
         ident_bf16 = keep.tile([P, P], BF16)
         masks.make_identity(nc, ident_bf16[:])
@@ -113,10 +115,12 @@ def tile_attention_before_s_kernel(
         acc_tiles = []
 
         def regroup(n):
-            i, first, width = pieces[n]
+            t, first, width = pieces[n]
             vector_cols = width * VECTOR_EIGHTHS // 8
-            raw = raw_matrices[i // TILES_PER_MATRIX]
-            first += (i % TILES_PER_MATRIX) * N_TILE
+            load_first, raw = [
+                (lf, tile) for lf, lw, tile in loads[t] if lf <= first and first + width <= lf + lw
+            ][0]
+            first -= load_first
             grouped = stream.tile([P, width, PACK], BF16, align_bytes=64)
             for copy, lo, hi in (
                 (nc.vector.tensor_copy, 0, vector_cols),
@@ -152,9 +156,7 @@ def tile_attention_before_s_kernel(
             acc_tiles.append(acc)
 
         def add_bias_and_store(n):
-            i, first, width = pieces[n]
-            t = i // TILES_PER_MATRIX
-            column = (i % TILES_PER_MATRIX) * N_TILE + first
+            t, column, width = pieces[n]
             result = stream.tile([P, width], F32)
             nc.vector.tensor_tensor(
                 out=result[:],
@@ -169,15 +171,13 @@ def tile_attention_before_s_kernel(
                     in_=result[b:P:BATCH, :].rearrange("s (h d) -> s h d", d=HEAD_DIM),
                 )
 
-        regroup(0)
-        spread_bias(0)
         quantise_tokens()
-        for step in range(1, n_pieces + 2):
+        for step in range(n_pieces + 2):
             if step < n_pieces:
                 regroup(step)
-            if step < len(biases):
-                spread_bias(step)
-            if step - 1 < n_pieces:
+            if step in first_piece:
+                spread_bias(first_piece.index(step))
+            if 1 <= step <= n_pieces:
                 quantise_and_multiply(step - 1)
             if step >= 2:
                 add_bias_and_store(step - 2)

@@ -23,7 +23,7 @@ LOAD_WIDTHS = ((256, 256, 512), (512, 512), (512, 512))
 
 PIECE_WIDTHS = ((256, 256, 512), (512, 512), (512, 256, 128, 128))
 
-VECTOR_EIGHTHS = 3
+VECTOR_SIXTEENTHS = 7
 
 assert HIDDEN == P * PACK and TOKENS == P
 
@@ -116,7 +116,7 @@ def tile_attention_before_s_kernel(
 
         def regroup(n):
             t, first, width = pieces[n]
-            vector_cols = width * VECTOR_EIGHTHS // 8
+            vector_cols = width * VECTOR_SIXTEENTHS // 16
             load_first, raw = [
                 (lf, tile) for lf, lw, tile in loads[t] if lf <= first and first + width <= lf + lw
             ][0]

@@ -43,7 +43,7 @@ def tile_attention_before_s_kernel(
         for j, width in enumerate(widths):
             pieces.append((t, sum(widths[:j]), width))
     n_pieces = len(pieces)
-    first_piece = [sum(len(w) for w in PIECE_WIDTHS[:t]) for t in range(len(weights))]
+    spread_steps = [max(1, sum(len(w) for w in PIECE_WIDTHS[:t])) for t in range(len(weights))]
 
     with ExitStack() as ctx:
         keep = ctx.enter_context(tc.tile_pool(name="keep", bufs=1))
@@ -53,6 +53,8 @@ def tile_attention_before_s_kernel(
         psum_acc = ctx.enter_context(tc.psum_pool(name="psum_acc", bufs=4))
         ctx.enter_context(tc.manual_schedule())
 
+        x_sb = keep.tile([P, HIDDEN], BF16)
+        nc.sync.dma_start(out=x_sb[:], in_=hidden_states.rearrange("b s k -> s b k"))
         bias_rows = keep.tile([P, P], BF16)
         nc.vector.memset(bias_rows[:], 0.0)
         for t, bias in enumerate(biases):
@@ -60,8 +62,6 @@ def tile_attention_before_s_kernel(
                 out=bias_rows[t * BIAS_ROWS : (t + 1) * BIAS_ROWS, :],
                 in_=bias.rearrange("(r c) -> r c", c=P),
             )
-        x_sb = keep.tile([P, HIDDEN], BF16)
-        nc.sync.dma_start(out=x_sb[:], in_=hidden_states.rearrange("b s k -> s b k"))
         loads = []
         for t, widths in enumerate(LOAD_WIDTHS):
             loads.append([])
@@ -74,16 +74,18 @@ def tile_attention_before_s_kernel(
                 )
                 loads[t].append((first, width, raw))
 
-        ident_bf16 = keep.tile([P, P], BF16)
-        masks.make_identity(nc, ident_bf16[:])
         ident_f32 = keep.tile([P, P], F32)
         masks.make_identity(nc, ident_f32[:])
+        ident_bf16 = keep.tile([P, P], BF16)
+        masks.make_identity(nc, ident_bf16[:])
 
-        bias_t = psum_prep.tile([P, P], BF16)
-        nc.tensor.transpose(bias_t[:], bias_rows[:], ident_bf16[:])
         bias_cols = keep.tile([P, len(biases) * BIAS_ROWS], BF16)
-        nc.vector.tensor_copy(out=bias_cols[:], in_=bias_t[:, 0 : len(biases) * BIAS_ROWS])
         bias_all = keep.tile([P, len(biases), WIDTH], BF16)
+
+        def bias_columns():
+            bias_t = psum_prep.tile([P, P], BF16)
+            nc.tensor.transpose(bias_t[:], bias_rows[:], ident_bf16[:])
+            nc.vector.tensor_copy(out=bias_cols[:], in_=bias_t[:, 0 : len(biases) * BIAS_ROWS])
 
         def spread_bias(t):
             spread = psum_bias.tile([P, WIDTH], BF16)
@@ -97,16 +99,19 @@ def tile_attention_before_s_kernel(
         x_codes = keep.tile([P, TOKENS], U32, align_bytes=64)
         x_scales = keep.tile([P, TOKENS], U8, align_bytes=64)
 
-        def quantise_tokens():
+        x_grouped = keep.tile([P, TOKENS * PACK], BF16, align_bytes=64)
+
+        def transpose_tokens():
             x_words = x_sb[:].bitcast(F32).rearrange("t (p u) -> t u p", u=2)
             x_t = psum_prep.tile([P, 2, TOKENS], F32)
             for u in range(2):
                 nc.tensor.transpose(x_t[:, u, :], x_words[:, u, :], ident_f32[:])
-            x_grouped = keep.tile([P, TOKENS * PACK], BF16, align_bytes=64)
             nc.vector.tensor_copy(
                 out=x_grouped[:].bitcast(F32).rearrange("p (t u) -> p t u", u=2),
                 in_=x_t[:].rearrange("p u t -> p t u"),
             )
+
+        def quantise_tokens():
             nc.vector.quantize_mx(
                 out=x_codes[:].bitcast(FP8X4), scales=x_scales[:], in_=x_grouped[:]
             )
@@ -171,12 +176,16 @@ def tile_attention_before_s_kernel(
                     in_=result[b:P:BATCH, :].rearrange("s (h d) -> s h d", d=HEAD_DIM),
                 )
 
-        quantise_tokens()
         for step in range(n_pieces + 2):
+            if step == 0:
+                transpose_tokens()
+                bias_columns()
             if step < n_pieces:
                 regroup(step)
-            if step in first_piece:
-                spread_bias(first_piece.index(step))
+            if step == 0:
+                quantise_tokens()
+            if step in spread_steps:
+                spread_bias(spread_steps.index(step))
             if 1 <= step <= n_pieces:
                 quantise_and_multiply(step - 1)
             if step >= 2:

@@ -17,7 +17,7 @@ WIDTH = HEADS * HEAD_DIM
 TOKENS = BATCH * SEQ
 N_TILE = 512
 BIAS_ROWS = WIDTH // P
-RUN = 4
+RUN = 8
 
 LOAD_WIDTHS = ((256, 256, 512), (512, 512), (512, 512))
 
@@ -121,7 +121,7 @@ def tile_attention_before_s_kernel(
 
         def regroup(n):
             t, first, width = pieces[n]
-            vector_cols = width * VECTOR_SIXTEENTHS // 16
+            vector_cols = width * VECTOR_SIXTEENTHS // 16 // (2 * RUN) * (2 * RUN)
             load_first, raw = [
                 (lf, tile) for lf, lw, tile in loads[t] if lf <= first and first + width <= lf + lw
             ][0]

@@ -16,7 +16,8 @@ HEADS, HEAD_DIM = 16, 64
 WIDTH = HEADS * HEAD_DIM
 TOKENS = BATCH * SEQ
 N_TILE = 512
-BIAS_ROWS = WIDTH // P
+BIAS_ROW = 2 * P
+BIAS_ROWS = WIDTH // BIAS_ROW
 RUN = 8
 
 LOAD_WIDTHS = ((256, 256, 512), (512, 512), (512, 512))
@@ -43,7 +44,7 @@ def tile_attention_before_s_kernel(
         for j, width in enumerate(widths):
             pieces.append((t, sum(widths[:j]), width))
     n_pieces = len(pieces)
-    spread_steps = [max(1, sum(len(w) for w in PIECE_WIDTHS[:t])) for t in range(len(weights))]
+    bias_steps = [max(1, sum(len(w) for w in PIECE_WIDTHS[:t])) for t in range(len(weights))]
 
     with ExitStack() as ctx:
         keep = ctx.enter_context(tc.tile_pool(name="keep", bufs=1))
@@ -55,12 +56,12 @@ def tile_attention_before_s_kernel(
 
         x_sb = keep.tile([P, HIDDEN], BF16)
         nc.sync.dma_start(out=x_sb[:], in_=hidden_states.rearrange("b s k -> s b k"))
-        bias_rows = keep.tile([P, P], BF16)
+        bias_rows = keep.tile([P, BIAS_ROW], BF16)
         nc.vector.memset(bias_rows[:], 0.0)
         for t, bias in enumerate(biases):
             nc.sync.dma_start(
                 out=bias_rows[t * BIAS_ROWS : (t + 1) * BIAS_ROWS, :],
-                in_=bias.rearrange("(r c) -> r c", c=P),
+                in_=bias.rearrange("(r c) -> r c", c=BIAS_ROW),
             )
         loads = []
         for t, widths in enumerate(LOAD_WIDTHS):
@@ -76,25 +77,27 @@ def tile_attention_before_s_kernel(
 
         ident_f32 = keep.tile([P, P], F32)
         masks.make_identity(nc, ident_f32[:])
-        ident_bf16 = keep.tile([P, P], BF16)
-        masks.make_identity(nc, ident_bf16[:])
 
-        bias_cols = keep.tile([P, len(biases) * BIAS_ROWS], BF16)
+        bias_cols = keep.tile([P, len(biases) * BIAS_ROWS], F32)
         bias_all = keep.tile([P, len(biases), WIDTH], BF16)
+        spread_tiles = []
 
         def bias_columns():
-            bias_t = psum_prep.tile([P, P], BF16)
-            nc.tensor.transpose(bias_t[:], bias_rows[:], ident_bf16[:])
+            bias_t = psum_prep.tile([P, P], F32)
+            nc.tensor.transpose(bias_t[:], bias_rows[:].bitcast(F32), ident_f32[:])
             nc.vector.tensor_copy(out=bias_cols[:], in_=bias_t[:, 0 : len(biases) * BIAS_ROWS])
 
         def spread_bias(t):
-            spread = psum_bias.tile([P, WIDTH], BF16)
+            spread = psum_bias.tile([P, WIDTH // 2], F32)
             for r in range(BIAS_ROWS):
                 column = bias_cols[:, t * BIAS_ROWS + r : t * BIAS_ROWS + r + 1]
                 nc.tensor.transpose(
-                    spread[:, r * P : (r + 1) * P], column.to_broadcast([P, P]), ident_bf16[:]
+                    spread[:, r * P : (r + 1) * P], column.to_broadcast([P, P]), ident_f32[:]
                 )
-            nc.scalar.copy(out=bias_all[:, t, :], in_=spread[:])
+            spread_tiles.append(spread)
+
+        def keep_bias(t):
+            nc.scalar.copy(out=bias_all[:, t, :], in_=spread_tiles[t][:].bitcast(BF16))
 
         x_codes = keep.tile([P, TOKENS], U32, align_bytes=64)
         x_scales = keep.tile([P, TOKENS], U8, align_bytes=64)
@@ -184,8 +187,10 @@ def tile_attention_before_s_kernel(
                 regroup(step)
             if step == 0:
                 quantise_tokens()
-            if step in spread_steps:
-                spread_bias(spread_steps.index(step))
+            if 1 <= step <= len(biases):
+                spread_bias(step - 1)
+            if step in bias_steps:
+                keep_bias(bias_steps.index(step))
             if 1 <= step <= n_pieces:
                 quantise_and_multiply(step - 1)
             if step >= 2:

@@ -142,6 +142,19 @@ def tile_attention_before_s_kernel(
                 )
             grouped_tiles.append(grouped)
 
+        weight_tiles = []
+
+        def multiply(out, codes, scales):
+            nc.tensor.matmul_mx(
+                out=out[:],
+                lhsT=x_codes[:].bitcast(FP8X4),
+                lhsT_scale=x_scales[:],
+                rhs=codes[:].bitcast(FP8X4),
+                rhs_scale=scales[:],
+                start=True,
+                stop=True,
+            )
+
         def quantise_and_multiply(n):
             width = pieces[n][2]
             codes = stream.tile([P, width], U32, align_bytes=64)
@@ -151,17 +164,13 @@ def tile_attention_before_s_kernel(
                 scales=scales[:],
                 in_=grouped_tiles[n][:].rearrange("p n j -> p (n j)"),
             )
+            weight_tiles.append((width, codes, scales))
             acc = psum_acc.tile([P, width], F32)
-            nc.tensor.matmul_mx(
-                out=acc[:],
-                lhsT=x_codes[:].bitcast(FP8X4),
-                lhsT_scale=x_scales[:],
-                rhs=codes[:].bitcast(FP8X4),
-                rhs_scale=scales[:],
-                start=True,
-                stop=True,
-            )
+            multiply(acc, codes, scales)
             acc_tiles.append(acc)
+            widest = max(weight_tiles, key=lambda tile: tile[0])
+            idle = psum_prep.tile([P, widest[0]], F32, name="x_t")
+            multiply(idle, widest[1], widest[2])
 
         def add_bias_and_store(n):
             t, column, width = pieces[n]

@@ -87,14 +87,16 @@ def tile_attention_before_s_kernel(
             nc.tensor.transpose(bias_t[:], bias_rows[:].bitcast(F32), ident_f32[:])
             nc.vector.tensor_copy(out=bias_cols[:], in_=bias_t[:, 0 : len(biases) * BIAS_ROWS])
 
-        def spread_bias(t):
-            spread = psum_bias.tile([P, WIDTH // 2], F32)
-            for r in range(BIAS_ROWS):
+        def spread_bias(t, rows):
+            if len(spread_tiles) == t:
+                spread_tiles.append(psum_bias.tile([P, WIDTH // 2], F32, name="spread"))
+            for r in rows:
                 column = bias_cols[:, t * BIAS_ROWS + r : t * BIAS_ROWS + r + 1]
                 nc.tensor.transpose(
-                    spread[:, r * P : (r + 1) * P], column.to_broadcast([P, P]), ident_f32[:]
+                    spread_tiles[t][:, r * P : (r + 1) * P],
+                    column.to_broadcast([P, P]),
+                    ident_f32[:],
                 )
-            spread_tiles.append(spread)
 
         def keep_bias(t):
             nc.scalar.copy(out=bias_all[:, t, :], in_=spread_tiles[t][:].bitcast(BF16))
@@ -125,6 +127,8 @@ def tile_attention_before_s_kernel(
         def regroup(n):
             t, first, width = pieces[n]
             vector_cols = width * VECTOR_SIXTEENTHS // 16 // (2 * RUN) * (2 * RUN)
+            if width == P:
+                vector_cols = 0
             load_first, raw = [
                 (lf, tile) for lf, lw, tile in loads[t] if lf <= first and first + width <= lf + lw
             ][0]
@@ -134,6 +138,8 @@ def tile_attention_before_s_kernel(
                 (nc.vector.tensor_copy, 0, vector_cols),
                 (nc.scalar.copy, vector_cols, width),
             ):
+                if lo == hi:
+                    continue
                 copy(
                     out=grouped[:, lo:hi, :].rearrange("p (c i) j -> p c j i", i=RUN),
                     in_=raw[:, :, first + lo : first + hi].rearrange(
@@ -196,11 +202,17 @@ def tile_attention_before_s_kernel(
                 regroup(step)
             if step == 0:
                 quantise_tokens()
-            if 1 <= step <= len(biases):
-                spread_bias(step - 1)
+            if step == 1:
+                spread_bias(0, range(BIAS_ROWS))
             if step in bias_steps:
                 keep_bias(bias_steps.index(step))
-            if 1 <= step <= n_pieces:
+            if 1 <= step < n_pieces:
                 quantise_and_multiply(step - 1)
+            if step == n_pieces - 1:
+                quantise_and_multiply(step)
+            if 1 <= step <= 4:
+                half = BIAS_ROWS // 2
+                first_row = (step - 1) % 2 * half
+                spread_bias((step + 1) // 2, range(first_row, first_row + half))
             if step >= 2:
                 add_bias_and_store(step - 2)

@@ -44,7 +44,7 @@ def tile_attention_before_s_kernel(
         for j, width in enumerate(widths):
             pieces.append((t, sum(widths[:j]), width))
     n_pieces = len(pieces)
-    bias_steps = [max(1, sum(len(w) for w in PIECE_WIDTHS[:t])) for t in range(len(weights))]
+    bias_steps = [sum(len(w) for w in PIECE_WIDTHS[:t]) for t in range(len(weights))]
 
     with ExitStack() as ctx:
         keep = ctx.enter_context(tc.tile_pool(name="keep", bufs=1))
@@ -58,11 +58,14 @@ def tile_attention_before_s_kernel(
         nc.sync.dma_start(out=x_sb[:], in_=hidden_states.rearrange("b s k -> s b k"))
         bias_rows = keep.tile([P, BIAS_ROW], BF16)
         nc.vector.memset(bias_rows[:], 0.0)
-        for t, bias in enumerate(biases):
-            nc.sync.dma_start(
-                out=bias_rows[t * BIAS_ROWS : (t + 1) * BIAS_ROWS, :],
-                in_=bias.rearrange("(r c) -> r c", c=BIAS_ROW),
-            )
+
+        def load_biases():
+            for b, bias in enumerate(biases):
+                nc.sync.dma_start(
+                    out=bias_rows[b * BIAS_ROWS : (b + 1) * BIAS_ROWS, :],
+                    in_=bias.rearrange("(r c) -> r c", c=BIAS_ROW),
+                )
+
         loads = []
         for t, widths in enumerate(LOAD_WIDTHS):
             loads.append([])
@@ -74,6 +77,8 @@ def tile_attention_before_s_kernel(
                     in_=weights[t][:, first : first + width].rearrange("(p j) n -> p j n", j=PACK),
                 )
                 loads[t].append((first, width, raw))
+                if (t, j) == (0, 0):
+                    load_biases()
 
         ident_f32 = keep.tile([P, P], F32)
         masks.make_identity(nc, ident_f32[:])
@@ -81,6 +86,25 @@ def tile_attention_before_s_kernel(
         bias_cols = keep.tile([P, len(biases) * BIAS_ROWS], F32)
         bias_all = keep.tile([P, len(biases), WIDTH], BF16)
         spread_tiles = []
+        selectors = keep.tile([P, BIAS_ROWS, P], BF16)
+        nc.vector.tensor_copy(
+            out=selectors[:],
+            in_=ident_f32[:, 0:BIAS_ROWS].unsqueeze(2).to_broadcast([P, BIAS_ROWS, P]),
+        )
+
+        def spread_first_bias():
+            half = BIAS_ROWS // 2
+            for first_row in range(0, BIAS_ROWS, half):
+                spread = psum_bias.tile([P, half, BIAS_ROW], BF16)
+                for r in range(half):
+                    nc.tensor.matmul(
+                        spread[:, r, :],
+                        lhsT=selectors[:, first_row + r, :],
+                        rhs=bias_rows[:],
+                        start=True,
+                        stop=True,
+                    )
+                spread_tiles.append(spread[:].rearrange("p r c -> p (r c)"))
 
         def bias_columns():
             bias_t = psum_prep.tile([P, P], F32)
@@ -88,18 +112,23 @@ def tile_attention_before_s_kernel(
             nc.vector.tensor_copy(out=bias_cols[:], in_=bias_t[:, 0 : len(biases) * BIAS_ROWS])
 
         def spread_bias(t, rows):
-            if len(spread_tiles) == t:
-                spread_tiles.append(psum_bias.tile([P, WIDTH // 2], F32, name="spread"))
+            if rows[0] == 0:
+                spread = psum_bias.tile([P, WIDTH // 2], F32)
+                spread_tiles.append(spread[:])
             for r in rows:
                 column = bias_cols[:, t * BIAS_ROWS + r : t * BIAS_ROWS + r + 1]
                 nc.tensor.transpose(
-                    spread_tiles[t][:, r * P : (r + 1) * P],
+                    spread_tiles[-1][:, r * P : (r + 1) * P],
                     column.to_broadcast([P, P]),
                     ident_f32[:],
                 )
 
+        def keep_first_bias(half):
+            columns = slice(half * WIDTH // 2, (half + 1) * WIDTH // 2)
+            nc.scalar.copy(out=bias_all[:, 0, columns], in_=spread_tiles[half])
+
         def keep_bias(t):
-            nc.scalar.copy(out=bias_all[:, t, :], in_=spread_tiles[t][:].bitcast(BF16))
+            nc.scalar.copy(out=bias_all[:, t, :], in_=spread_tiles[t + 1].bitcast(BF16))
 
         x_codes = keep.tile([P, TOKENS], U32, align_bytes=64)
         x_scales = keep.tile([P, TOKENS], U8, align_bytes=64)
@@ -197,14 +226,15 @@ def tile_attention_before_s_kernel(
         for step in range(n_pieces + 2):
             if step == 0:
                 transpose_tokens()
-                bias_columns()
             if step < n_pieces:
                 regroup(step)
             if step == 0:
+                bias_columns()
+                spread_first_bias()
                 quantise_tokens()
-            if step == 1:
-                spread_bias(0, range(BIAS_ROWS))
-            if step in bias_steps:
+            if step in (1, 2):
+                keep_first_bias(step - 1)
+            if step in bias_steps[1:]:
                 keep_bias(bias_steps.index(step))
             if 1 <= step < n_pieces:
                 quantise_and_multiply(step - 1)

@@ -24,7 +24,7 @@ LOAD_WIDTHS = ((256, 256, 512), (512, 512), (512, 512))
 
 PIECE_WIDTHS = ((256, 256, 512), (512, 512), (512, 256, 128, 128))
 
-VECTOR_SIXTEENTHS = 7
+VECTOR_SIXTEENTHS = (8, 7, 6)
 
 assert HIDDEN == P * PACK and TOKENS == P
 
@@ -44,6 +44,7 @@ def tile_attention_before_s_kernel(
         for j, width in enumerate(widths):
             pieces.append((t, sum(widths[:j]), width))
     n_pieces = len(pieces)
+    last_wide = max(n for n in range(n_pieces) if pieces[n][2] == N_TILE)
     bias_steps = [sum(len(w) for w in PIECE_WIDTHS[:t]) for t in range(len(weights))]
 
     with ExitStack() as ctx:
@@ -155,7 +156,7 @@ def tile_attention_before_s_kernel(
 
         def regroup(n):
             t, first, width = pieces[n]
-            vector_cols = width * VECTOR_SIXTEENTHS // 16 // (2 * RUN) * (2 * RUN)
+            vector_cols = width * VECTOR_SIXTEENTHS[t] // 16 // (2 * RUN) * (2 * RUN)
             if width == P:
                 vector_cols = 0
             load_first, raw = [
@@ -226,6 +227,8 @@ def tile_attention_before_s_kernel(
         for step in range(n_pieces + 2):
             if step == 0:
                 transpose_tokens()
+            if step == last_wide + 1:
+                quantise_and_multiply(last_wide)
             if step < n_pieces:
                 regroup(step)
             if step == 0:
@@ -236,7 +239,7 @@ def tile_attention_before_s_kernel(
                 keep_first_bias(step - 1)
             if step in bias_steps[1:]:
                 keep_bias(bias_steps.index(step))
-            if 1 <= step < n_pieces:
+            if 1 <= step < n_pieces and step != last_wide + 1:
                 quantise_and_multiply(step - 1)
             if step == n_pieces - 1:
                 quantise_and_multiply(step)

@@ -26,6 +26,8 @@ PIECE_WIDTHS = ((256, 256, 512), (512, 512), (512, 256, 128, 128))
 
 VECTOR_SIXTEENTHS = (8, 7, 6)
 
+IDLE_BANKS = ("x_t", "bias_t")
+
 assert HIDDEN == P * PACK and TOKENS == P
 
 FLOPS = 2 * TOKENS * HIDDEN * 3 * WIDTH
@@ -204,9 +206,11 @@ def tile_attention_before_s_kernel(
             acc = psum_acc.tile([P, width], F32)
             multiply(acc, codes, scales)
             acc_tiles.append(acc)
-            widest = max(weight_tiles, key=lambda tile: tile[0])
-            idle = psum_prep.tile([P, widest[0]], F32, name="x_t")
-            multiply(idle, widest[1], widest[2])
+            if n < n_pieces - 2:
+                widest = max(weight_tiles, key=lambda tile: tile[0])
+                for bank in IDLE_BANKS:
+                    idle = psum_prep.tile([P, widest[0]], F32, name=bank)
+                    multiply(idle, widest[1], widest[2])
 
         def add_bias_and_store(n):
             t, column, width = pieces[n]

from contextlib import ExitStack

import concourse.masks as masks
import concourse.mybir as mybir

BF16 = mybir.dt.bfloat16
F32 = mybir.dt.float32
U32 = mybir.dt.uint32
U8 = mybir.dt.uint8
FP8X4 = mybir.dt.float8_e4m3fn_x4

P = 128
PACK = 4
BATCH, SEQ, HIDDEN = 2, 64, 512
HEADS, HEAD_DIM = 16, 64
WIDTH = HEADS * HEAD_DIM
TOKENS = BATCH * SEQ
N_TILE = 512
BIAS_ROW = 2 * P
BIAS_ROWS = WIDTH // BIAS_ROW
RUN = 8

LOAD_WIDTHS = ((256, 256, 512), (512, 512), (512, 512))

PIECE_WIDTHS = ((256, 256, 512), (512, 512), (512, 256, 128, 128))

VECTOR_SIXTEENTHS = (8, 7, 6)

IDLE_BANKS = ("x_t", "bias_t")

assert HIDDEN == P * PACK and TOKENS == P

FLOPS = 2 * TOKENS * HIDDEN * 3 * WIDTH


def tile_attention_before_s_kernel(
    tc, hidden_states, Wq, bq, Wk, bk, Wv, bv, out_0, out_1, out_2
):
    nc = tc.nc
    weights = (Wq, Wk, Wv)
    biases = (bq, bk, bv)
    outs = (out_0, out_1, out_2)

    pieces = []
    for t, widths in enumerate(PIECE_WIDTHS):
        for j, width in enumerate(widths):
            pieces.append((t, sum(widths[:j]), width))
    n_pieces = len(pieces)
    last_wide = max(n for n in range(n_pieces) if pieces[n][2] == N_TILE)
    bias_steps = [sum(len(w) for w in PIECE_WIDTHS[:t]) for t in range(len(weights))]

    with ExitStack() as ctx:
        keep = ctx.enter_context(tc.tile_pool(name="keep", bufs=1))
        stream = ctx.enter_context(tc.tile_pool(name="stream", bufs=n_pieces))
        psum_prep = ctx.enter_context(tc.psum_pool(name="psum_prep", bufs=1))
        psum_bias = ctx.enter_context(tc.psum_pool(name="psum_bias", bufs=2))
        psum_acc = ctx.enter_context(tc.psum_pool(name="psum_acc", bufs=4))
        ctx.enter_context(tc.manual_schedule())

        x_sb = keep.tile([P, HIDDEN], BF16)
        nc.sync.dma_start(out=x_sb[:], in_=hidden_states.rearrange("b s k -> s b k"))
        bias_rows = keep.tile([P, BIAS_ROW], BF16)
        nc.vector.memset(bias_rows[:], 0.0)

        def load_biases():
            for b, bias in enumerate(biases):
                nc.sync.dma_start(
                    out=bias_rows[b * BIAS_ROWS : (b + 1) * BIAS_ROWS, :],
                    in_=bias.rearrange("(r c) -> r c", c=BIAS_ROW),
                )

        loads = []
        for t, widths in enumerate(LOAD_WIDTHS):
            loads.append([])
            for j, width in enumerate(widths):
                first = sum(widths[:j])
                raw = keep.tile([P, PACK, width], BF16, name="raw%d_%d" % (t, j))
                nc.sync.dma_start(
                    out=raw[:],
                    in_=weights[t][:, first : first + width].rearrange("(p j) n -> p j n", j=PACK),
                )
                loads[t].append((first, width, raw))
                if (t, j) == (0, 0):
                    load_biases()

        ident_f32 = keep.tile([P, P], F32)
        masks.make_identity(nc, ident_f32[:])

        bias_cols = keep.tile([P, len(biases) * BIAS_ROWS], F32)
        bias_all = keep.tile([P, len(biases), WIDTH], BF16)
        spread_tiles = []
        selectors = keep.tile([P, BIAS_ROWS, P], BF16)
        nc.vector.tensor_copy(
            out=selectors[:],
            in_=ident_f32[:, 0:BIAS_ROWS].unsqueeze(2).to_broadcast([P, BIAS_ROWS, P]),
        )

        def spread_first_bias():
            half = BIAS_ROWS // 2
            for first_row in range(0, BIAS_ROWS, half):
                spread = psum_bias.tile([P, half, BIAS_ROW], BF16)
                for r in range(half):
                    nc.tensor.matmul(
                        spread[:, r, :],
                        lhsT=selectors[:, first_row + r, :],
                        rhs=bias_rows[:],
                        start=True,
                        stop=True,
                    )
                spread_tiles.append(spread[:].rearrange("p r c -> p (r c)"))

        def bias_columns():
            bias_t = psum_prep.tile([P, P], F32)
            nc.tensor.transpose(bias_t[:], bias_rows[:].bitcast(F32), ident_f32[:])
            nc.vector.tensor_copy(out=bias_cols[:], in_=bias_t[:, 0 : len(biases) * BIAS_ROWS])

        def spread_bias(t, rows):
            if rows[0] == 0:
                spread = psum_bias.tile([P, WIDTH // 2], F32)
                spread_tiles.append(spread[:])
            for r in rows:
                column = bias_cols[:, t * BIAS_ROWS + r : t * BIAS_ROWS + r + 1]
                nc.tensor.transpose(
                    spread_tiles[-1][:, r * P : (r + 1) * P],
                    column.to_broadcast([P, P]),
                    ident_f32[:],
                )

        def keep_first_bias(half):
            columns = slice(half * WIDTH // 2, (half + 1) * WIDTH // 2)
            nc.scalar.copy(out=bias_all[:, 0, columns], in_=spread_tiles[half])

        def keep_bias(t):
            nc.scalar.copy(out=bias_all[:, t, :], in_=spread_tiles[t + 1].bitcast(BF16))

        x_codes = keep.tile([P, TOKENS], U32, align_bytes=64)
        x_scales = keep.tile([P, TOKENS], U8, align_bytes=64)

        x_grouped = keep.tile([P, TOKENS * PACK], BF16, align_bytes=64)

        def transpose_tokens():
            x_words = x_sb[:].bitcast(F32).rearrange("t (p u) -> t u p", u=2)
            x_t = psum_prep.tile([P, 2, TOKENS], F32)
            for u in range(2):
                nc.tensor.transpose(x_t[:, u, :], x_words[:, u, :], ident_f32[:])
            nc.vector.tensor_copy(
                out=x_grouped[:].bitcast(F32).rearrange("p (t u) -> p t u", u=2),
                in_=x_t[:].rearrange("p u t -> p t u"),
            )

        def quantise_tokens():
            nc.vector.quantize_mx(
                out=x_codes[:].bitcast(FP8X4), scales=x_scales[:], in_=x_grouped[:]
            )

        grouped_tiles = []
        acc_tiles = []

        def regroup(n):
            t, first, width = pieces[n]
            vector_cols = width * VECTOR_SIXTEENTHS[t] // 16 // (2 * RUN) * (2 * RUN)
            if width == P:
                vector_cols = 0
            load_first, raw = [
                (lf, tile) for lf, lw, tile in loads[t] if lf <= first and first + width <= lf + lw
            ][0]
            first -= load_first
            grouped = stream.tile([P, width, PACK], BF16, align_bytes=64)
            for copy, lo, hi in (
                (nc.vector.tensor_copy, 0, vector_cols),
                (nc.scalar.copy, vector_cols, width),
            ):
                if lo == hi:
                    continue
                copy(
                    out=grouped[:, lo:hi, :].rearrange("p (c i) j -> p c j i", i=RUN),
                    in_=raw[:, :, first + lo : first + hi].rearrange(
                        "p j (c i) -> p c j i", i=RUN
                    ),
                )
            grouped_tiles.append(grouped)

        weight_tiles = []

        def multiply(out, codes, scales):
            nc.tensor.matmul_mx(
                out=out[:],
                lhsT=x_codes[:].bitcast(FP8X4),
                lhsT_scale=x_scales[:],
                rhs=codes[:].bitcast(FP8X4),
                rhs_scale=scales[:],
                start=True,
                stop=True,
            )

        def quantise_and_multiply(n):
            width = pieces[n][2]
            codes = stream.tile([P, width], U32, align_bytes=64)
            scales = stream.tile([P, width], U8, align_bytes=64)
            nc.vector.quantize_mx(
                out=codes[:].bitcast(FP8X4),
                scales=scales[:],
                in_=grouped_tiles[n][:].rearrange("p n j -> p (n j)"),
            )
            weight_tiles.append((width, codes, scales))
            acc = psum_acc.tile([P, width], F32)
            multiply(acc, codes, scales)
            acc_tiles.append(acc)
            if n < n_pieces - 2:
                widest = max(weight_tiles, key=lambda tile: tile[0])
                for bank in IDLE_BANKS:
                    idle = psum_prep.tile([P, widest[0]], F32, name=bank)
                    multiply(idle, widest[1], widest[2])

        def add_bias_and_store(n):
            t, column, width = pieces[n]
            result = stream.tile([P, width], F32)
            nc.vector.tensor_tensor(
                out=result[:],
                in0=acc_tiles[n][:],
                in1=bias_all[:, t, column : column + width],
                op=mybir.AluOpType.add,
            )
            heads = slice(column // HEAD_DIM, (column + width) // HEAD_DIM)
            for b in range(BATCH):
                nc.sync.dma_start(
                    out=outs[t][b, heads, :, :].rearrange("h s d -> s h d"),
                    in_=result[b:P:BATCH, :].rearrange("s (h d) -> s h d", d=HEAD_DIM),
                )

        for step in range(n_pieces + 2):
            if step == 0:
                transpose_tokens()
            if step == last_wide + 1:
                quantise_and_multiply(last_wide)
            if step < n_pieces:
                regroup(step)
            if step == 0:
                bias_columns()
                spread_first_bias()
                quantise_tokens()
            if step in (1, 2):
                keep_first_bias(step - 1)
            if step in bias_steps[1:]:
                keep_bias(bias_steps.index(step))
            if 1 <= step < n_pieces and step != last_wide + 1:
                quantise_and_multiply(step - 1)
            if step == n_pieces - 1:
                quantise_and_multiply(step)
            if 1 <= step <= 4:
                half = BIAS_ROWS // 2
                first_row = (step - 1) % 2 * half
                spread_bias((step + 1) // 2, range(first_row, first_row + half))
            if step >= 2:
                add_bias_and_store(step - 2)
